import numpy as np
import ml_dtypes

BF16 = ml_dtypes.bfloat16


def bf(x):
    return np.asarray(x, np.float32).astype(BF16)


def f32(x):
    return np.asarray(x, np.float32)


def f64(x):
    return np.asarray(x).astype(np.float64)


def striped(idx):
    return np.tile(idx.reshape(-1, 16).T, (8, 1))


C, E, S, N, Q = 256, 128, 512, 128, 3


def sigmoid(v):
    return 1.0 / (1.0 + np.exp(-v))


def setup_inputs():
    return {
        "base": f32(0.5 * np.random.standard_normal((C, S))),
        "x": bf(np.random.standard_normal((E, N))),
        "w_ih": bf(np.random.standard_normal((E, Q * C)) / np.sqrt(E)),
        "b_ih": f32(0.5 * np.random.standard_normal((Q * C, 1))),
        "b_hh": f32(0.5 * np.random.standard_normal((Q * C, 1))),
        "offs": striped(np.random.permutation(S)[:N]),
    }


def reference(base, x, w_ih, b_ih, b_hh, offs):
    idx = offs[:16].T.reshape(-1)
    a = f64(w_ih).T @ f64(x) + f64(b_ih)
    i_r, i_z, i_n = a.reshape(Q, C, N)
    h_r, h_z, h_n = f64(b_hh).reshape(Q, C, 1)
    r = sigmoid(i_r + h_r)
    z = sigmoid(i_z + h_z)
    n = np.tanh(i_n + r * h_n)
    out = f64(base).copy()
    out[:, idx] = (1.0 - z) * n
    return out

@@ -1,0 +1,101 @@
+import concourse.mybir as mybir
+
+F32, BF16, U16 = mybir.dt.float32, mybir.dt.bfloat16, mybir.dt.uint16
+MULT, ADD, SUBTRACT = mybir.AluOpType.mult, mybir.AluOpType.add, mybir.AluOpType.subtract
+SIGMOID, TANH = mybir.ActivationFunctionType.Sigmoid, mybir.ActivationFunctionType.Tanh
+
+P = 128
+C, E, S, N = 256, 128, 512, 128
+BLOCKS = C // P
+R, Z, NEW = 0, 1, 2
+GATES = 3
+IH, HH = 0, 1
+PIECES = (GATES - 1) * BLOCKS
+SQUARE = 32
+FLIPPED = PIECES * SQUARE
+
+FLOPS = 2 * E * GATES * C * N
+
+
+def tile_batchtreeencoder_kernel(tc, base, x, w_ih, b_ih, b_hh, offs, out):
+    nc = tc.nc
+    with tc.tile_pool(name="held", bufs=1) as held, tc.psum_pool(name="psum", bufs=1) as psum:
+        r_rows = held.tile([2 * BLOCKS, P], F32, name="r_rows")
+        for s, (queue, bias) in enumerate(((nc.sync, b_ih), (nc.scalar, b_hh))):
+            queue.dma_start(r_rows[s : 2 * BLOCKS : 2, :], bias[0:C, :].rearrange("(b c) o -> b (c o)", b=BLOCKS))
+        nodes = held.tile([E, N], BF16, name="nodes")
+        nc.scalar.dma_start(nodes[:], x)
+        weights = held.tile([E, GATES * C], BF16, name="weights")
+        nc.sync.dma_start(weights[:], w_ih)
+        bias_runs = held.tile([P, FLIPPED], F32, name="bias_runs", align_bytes=64)
+        nc.vector.memset(bias_runs[:], 0.0)
+        for s, (queue, bias) in enumerate(((nc.sync, b_ih), (nc.scalar, b_hh))):
+            queue.dma_start(
+                bias_runs[s:P:SQUARE, :].rearrange("i (k a) -> i k a", k=PIECES),
+                bias[C : GATES * C, :].rearrange("(k i a) o -> i k (a o)", k=PIECES, a=SQUARE),
+            )
+        offsets = held.tile([P, N // 16], U16, name="offsets")
+        nc.sync.dma_start(offsets[:], offs)
+        windows = [held.tile([P, S], F32, name=f"window{b}") for b in range(BLOCKS)]
+        for b in range(BLOCKS):
+            nc.sync.dma_start(windows[b][:], base[b * P : (b + 1) * P, :])
+
+        zero = held.tile([P, 1], F32, name="zero")
+        nc.vector.memset(zero[:], 0.0)
+        warmed = held.tile([P, 1], F32, name="warmed")
+        nc.scalar.activation(warmed[:], zero[:], SIGMOID)
+
+        pairs = held.tile([2 * BLOCKS, BLOCKS], F32, name="pairs")
+        nc.vector.memset(pairs[:, 0:1], 0.0)
+        nc.vector.memset(pairs[:, 1:2], 1.0)
+        nc.vector.memset(pairs[0:2, 0:1], 1.0)
+        nc.vector.memset(pairs[0:2, 1:2], 0.0)
+        upright_r = psum.tile([P, BLOCKS], F32, name="upright_r")
+        nc.tensor.matmul(upright_r[:], r_rows[:], pairs[:], start=True, stop=True)
+        bias_r = held.tile([P, BLOCKS], F32, name="bias_r")
+        nc.vector.tensor_copy(bias_r[:], upright_r[:])
+
+        biases = held.tile([P, FLIPPED], F32, name="biases", align_bytes=64)
+        nc.vector.transpose(biases[:], bias_runs[:])
+
+        def bias_of(s, gate, first_block=0, blocks=BLOCKS):
+            first = ((gate - 1) * BLOCKS + first_block) * SQUARE + s
+            return biases[:, first : first + (blocks - 1) * SQUARE + 1 : SQUARE]
+
+        minus_bias_z = held.tile([P, BLOCKS], F32, name="minus_bias_z")
+        nc.vector.scalar_tensor_tensor(minus_bias_z[:], bias_of(IH, Z), -1.0, bias_of(HH, Z), MULT, SUBTRACT)
+
+        products = {}
+        for b in range(BLOCKS):
+            for gate in (R, NEW, Z):
+                products[gate, b] = psum.tile([P, N], F32, name=f"product{gate}{b}")
+                first = gate * C + b * P
+                nc.tensor.matmul(products[gate, b][:], weights[:, first : first + P], nodes[:], start=True, stop=True)
+
+        pieces = ((0, 0, N // 2), (0, N // 2, N // 2), (1, 0, N))
+        reset = [held.tile([P, N], F32, name=f"reset{b}") for b in range(BLOCKS)]
+        for b, first, nodes_here in pieces:
+            here = slice(first, first + nodes_here)
+            nc.scalar.activation(
+                reset[b][:, here], products[R, b][:, here], SIGMOID, bias=bias_r[:, b : b + 1], scale=1.0
+            )
+        before_tanh = [held.tile([P, N], F32, name=f"before_tanh{b}") for b in range(BLOCKS)]
+        for b, first, nodes_here in pieces:
+            here = slice(first, first + nodes_here)
+            nc.vector.scalar_tensor_tensor(
+                before_tanh[b][:, here], reset[b][:, here], bias_of(HH, NEW, b, 1), products[NEW, b][:, here], MULT, ADD
+            )
+        one_minus_z = [held.tile([P, N], F32, name=f"one_minus_z{b}") for b in range(BLOCKS)]
+        for b in range(BLOCKS):
+            nc.scalar.activation(
+                one_minus_z[b][:], products[Z, b][:], SIGMOID, bias=minus_bias_z[:, b : b + 1], scale=-1.0
+            )
+        new = [held.tile([P, N], F32, name=f"new{b}") for b in range(BLOCKS)]
+        for b, first, nodes_here in pieces:
+            here = slice(first, first + nodes_here)
+            nc.scalar.activation(new[b][:, here], before_tanh[b][:, here], TANH, bias=bias_of(IH, NEW, b, 1), scale=1.0)
+
+        for b in range(BLOCKS):
+            nc.vector.tensor_tensor(windows[b][:].indirect(offsets[:]), one_minus_z[b][:], new[b][:], MULT)
+        nc.scalar.dma_start(out[0:P, :], windows[0][:])
+        nc.sync.dma_start(out[P : 2 * P, :], windows[1][:])

@@ -25,8 +25,10 @@ def tile_batchtreeencoder_kernel(tc, base, x, w_ih, b_ih, b_hh, offs, out):
             queue.dma_start(r_rows[s : 2 * BLOCKS : 2, :], bias[0:C, :].rearrange("(b c) o -> b (c o)", b=BLOCKS))
         nodes = held.tile([E, N], BF16, name="nodes")
         nc.scalar.dma_start(nodes[:], x)
-        weights = held.tile([E, GATES * C], BF16, name="weights")
-        nc.sync.dma_start(weights[:], w_ih)
+        weights_r = held.tile([E, C], BF16, name="weights_r")
+        nc.sync.dma_start(weights_r[:], w_ih[:, 0:C])
+        weights_zn = held.tile([E, (GATES - 1) * C], BF16, name="weights_zn")
+        nc.sync.dma_start(weights_zn[:], w_ih[:, C : GATES * C])
         bias_runs = held.tile([P, FLIPPED], F32, name="bias_runs", align_bytes=64)
         nc.vector.memset(bias_runs[:], 0.0)
         for s, (queue, bias) in enumerate(((nc.sync, b_ih), (nc.scalar, b_hh))):
@@ -66,11 +68,17 @@ def tile_batchtreeencoder_kernel(tc, base, x, w_ih, b_ih, b_hh, offs, out):
         nc.vector.scalar_tensor_tensor(minus_bias_z[:], bias_of(IH, Z), -1.0, bias_of(HH, Z), MULT, SUBTRACT)
 
         products = {}
+
+        def multiply(gate, b):
+            weights, first = (weights_r, b * P) if gate == R else (weights_zn, (gate - Z) * C + b * P)
+            products[gate, b] = psum.tile([P, N], F32, name=f"product{gate}{b}")
+            nc.tensor.matmul(products[gate, b][:], weights[:, first : first + P], nodes[:], start=True, stop=True)
+
         for b in range(BLOCKS):
-            for gate in (R, NEW, Z):
-                products[gate, b] = psum.tile([P, N], F32, name=f"product{gate}{b}")
-                first = gate * C + b * P
-                nc.tensor.matmul(products[gate, b][:], weights[:, first : first + P], nodes[:], start=True, stop=True)
+            multiply(R, b)
+        for b in range(BLOCKS):
+            for gate in (NEW, Z):
+                multiply(gate, b)
 
         pieces = ((0, 0, N // 2), (0, N // 2, N // 2), (1, 0, N))
         reset = [held.tile([P, N], F32, name=f"reset{b}") for b in range(BLOCKS)]

import concourse.mybir as mybir

F32, BF16, U16 = mybir.dt.float32, mybir.dt.bfloat16, mybir.dt.uint16
MULT, ADD, SUBTRACT = mybir.AluOpType.mult, mybir.AluOpType.add, mybir.AluOpType.subtract
SIGMOID, TANH = mybir.ActivationFunctionType.Sigmoid, mybir.ActivationFunctionType.Tanh

P = 128
C, E, S, N = 256, 128, 512, 128
BLOCKS = C // P
R, Z, NEW = 0, 1, 2
GATES = 3
IH, HH = 0, 1
PIECES = (GATES - 1) * BLOCKS
SQUARE = 32
FLIPPED = PIECES * SQUARE

FLOPS = 2 * E * GATES * C * N


def tile_batchtreeencoder_kernel(tc, base, x, w_ih, b_ih, b_hh, offs, out):
    nc = tc.nc
    with tc.tile_pool(name="held", bufs=1) as held, tc.psum_pool(name="psum", bufs=1) as psum:
        r_rows = held.tile([2 * BLOCKS, P], F32, name="r_rows")
        for s, (queue, bias) in enumerate(((nc.sync, b_ih), (nc.scalar, b_hh))):
            queue.dma_start(r_rows[s : 2 * BLOCKS : 2, :], bias[0:C, :].rearrange("(b c) o -> b (c o)", b=BLOCKS))
        nodes = held.tile([E, N], BF16, name="nodes")
        nc.scalar.dma_start(nodes[:], x)
        weights_r = held.tile([E, C], BF16, name="weights_r")
        nc.sync.dma_start(weights_r[:], w_ih[:, 0:C])
        weights_zn = held.tile([E, (GATES - 1) * C], BF16, name="weights_zn")
        nc.sync.dma_start(weights_zn[:], w_ih[:, C : GATES * C])
        bias_runs = held.tile([P, FLIPPED], F32, name="bias_runs", align_bytes=64)
        nc.vector.memset(bias_runs[:], 0.0)
        for s, (queue, bias) in enumerate(((nc.sync, b_ih), (nc.scalar, b_hh))):
            queue.dma_start(
                bias_runs[s:P:SQUARE, :].rearrange("i (k a) -> i k a", k=PIECES),
                bias[C : GATES * C, :].rearrange("(k i a) o -> i k (a o)", k=PIECES, a=SQUARE),
            )
        offsets = held.tile([P, N // 16], U16, name="offsets")
        nc.sync.dma_start(offsets[:], offs)
        windows = [held.tile([P, S], F32, name=f"window{b}") for b in range(BLOCKS)]
        for b in range(BLOCKS):
            nc.sync.dma_start(windows[b][:], base[b * P : (b + 1) * P, :])

        zero = held.tile([P, 1], F32, name="zero")
        nc.vector.memset(zero[:], 0.0)
        warmed = held.tile([P, 1], F32, name="warmed")
        nc.scalar.activation(warmed[:], zero[:], SIGMOID)

        pairs = held.tile([2 * BLOCKS, BLOCKS], F32, name="pairs")
        nc.vector.memset(pairs[:, 0:1], 0.0)
        nc.vector.memset(pairs[:, 1:2], 1.0)
        nc.vector.memset(pairs[0:2, 0:1], 1.0)
        nc.vector.memset(pairs[0:2, 1:2], 0.0)
        upright_r = psum.tile([P, BLOCKS], F32, name="upright_r")
        nc.tensor.matmul(upright_r[:], r_rows[:], pairs[:], start=True, stop=True)
        bias_r = held.tile([P, BLOCKS], F32, name="bias_r")
        nc.vector.tensor_copy(bias_r[:], upright_r[:])

        biases = held.tile([P, FLIPPED], F32, name="biases", align_bytes=64)
        nc.vector.transpose(biases[:], bias_runs[:])

        def bias_of(s, gate, first_block=0, blocks=BLOCKS):
            first = ((gate - 1) * BLOCKS + first_block) * SQUARE + s
            return biases[:, first : first + (blocks - 1) * SQUARE + 1 : SQUARE]

        minus_bias_z = held.tile([P, BLOCKS], F32, name="minus_bias_z")
        nc.vector.scalar_tensor_tensor(minus_bias_z[:], bias_of(IH, Z), -1.0, bias_of(HH, Z), MULT, SUBTRACT)

        products = {}

        def multiply(gate, b):
            weights, first = (weights_r, b * P) if gate == R else (weights_zn, (gate - Z) * C + b * P)
            products[gate, b] = psum.tile([P, N], F32, name=f"product{gate}{b}")
            nc.tensor.matmul(products[gate, b][:], weights[:, first : first + P], nodes[:], start=True, stop=True)

        for b in range(BLOCKS):
            multiply(R, b)
        for b in range(BLOCKS):
            for gate in (NEW, Z):
                multiply(gate, b)

        pieces = ((0, 0, N // 2), (0, N // 2, N // 2), (1, 0, N))
        reset = [held.tile([P, N], F32, name=f"reset{b}") for b in range(BLOCKS)]
        for b, first, nodes_here in pieces:
            here = slice(first, first + nodes_here)
            nc.scalar.activation(
                reset[b][:, here], products[R, b][:, here], SIGMOID, bias=bias_r[:, b : b + 1], scale=1.0
            )
        before_tanh = [held.tile([P, N], F32, name=f"before_tanh{b}") for b in range(BLOCKS)]
        for b, first, nodes_here in pieces:
            here = slice(first, first + nodes_here)
            nc.vector.scalar_tensor_tensor(
                before_tanh[b][:, here], reset[b][:, here], bias_of(HH, NEW, b, 1), products[NEW, b][:, here], MULT, ADD
            )
        one_minus_z = [held.tile([P, N], F32, name=f"one_minus_z{b}") for b in range(BLOCKS)]
        for b in range(BLOCKS):
            nc.scalar.activation(
                one_minus_z[b][:], products[Z, b][:], SIGMOID, bias=minus_bias_z[:, b : b + 1], scale=-1.0
            )
        new = [held.tile([P, N], F32, name=f"new{b}") for b in range(BLOCKS)]
        for b, first, nodes_here in pieces:
            here = slice(first, first + nodes_here)
            nc.scalar.activation(new[b][:, here], before_tanh[b][:, here], TANH, bias=bias_of(IH, NEW, b, 1), scale=1.0)

        for b in range(BLOCKS):
            nc.vector.tensor_tensor(windows[b][:].indirect(offsets[:]), one_minus_z[b][:], new[b][:], MULT)
        nc.scalar.dma_start(out[0:P, :], windows[0][:])
        nc.sync.dma_start(out[P : 2 * P, :], windows[1][:])
